import numpy as np
import ml_dtypes


def mxq(x, axis, fmt="e4m3"):
    dtype, down = {"e4m3": (ml_dtypes.float8_e4m3fn, 7), "e5m2": (ml_dtypes.float8_e5m2, 14)}[fmt]
    v = np.moveaxis(np.asarray(x, np.float32).astype(ml_dtypes.bfloat16).astype(np.float64), axis, -1)
    blocks = v.reshape(v.shape[:-1] + (-1, 32))
    amax = np.abs(blocks).max(-1, keepdims=True)
    byte = np.maximum(np.where(amax > 0, np.frexp(amax)[1] - 1 + 127, 0) - down, 1)
    scale = np.exp2(byte - 127.0)
    codes = (blocks / scale).astype(np.float32).astype(dtype).astype(np.float64)
    return np.moveaxis((codes * scale).reshape(v.shape), -1, axis)


WIDE = False


def mx_kscale(k):
    if not WIDE:
        return np.ones(k)
    levels = np.array([10, -10, 5, -5, 0])
    a = np.random.permutation(np.resize(levels, k // 512 * 4)).reshape(k // 512, 4)
    idx = np.arange(k)
    return np.exp2(a[idx // 512, idx % 128 // 32])


BF16 = ml_dtypes.bfloat16


def bf(x):
    return np.asarray(x, np.float32).astype(BF16)


def f64(x):
    return np.asarray(x).astype(np.float64)


B, H, L, E, QD = 16, 1, 128, 2048, 128
EPS = 1e-5


def build_decay_mask(num_heads, max_len):
    r = f64(np.arange(max_len))
    dec = np.array([1.0 - 2.0 ** (-5 - h) for h in range(num_heads)])
    expo = r[None, :] - r[:, None]
    return np.where(r[:, None] >= r[None, :], dec[:, None, None] ** expo[None], 0.0)


def setup_inputs():
    s = mx_kscale(E)
    kv = (0.1 + 0.32 * np.random.standard_normal((B, H, L, QD))) * (0.1 + 0.32 * np.random.standard_normal((B, H, L, QD)))
    return {"x": bf(np.random.standard_normal((B, H, L, E)) * s),
            "Wq": bf(np.random.standard_normal((QD, E)) / np.sqrt(E) / s),
            "bq": bf(0.3 + 0.3 * np.random.standard_normal(QD)),
            "kv": bf(kv),
            "decay_mask": bf(build_decay_mask(H, L))}


def reference(x, Wq, bq, kv, decay_mask):
    b, h, l, e = x.shape
    Q = (mxq(f64(x), 3, "e4m3") @ mxq(f64(Wq), 1, "e4m3").T) + f64(bq)
    D = f64(decay_mask)[0, :l, :l]
    y = Q * (f64(kv) @ D.T)
    mean = y.mean(axis=(2, 3), keepdims=True)
    var = ((y - mean) ** 2).mean(axis=(2, 3), keepdims=True)
    y = (y - mean) / np.sqrt(var + EPS)
    return y.reshape(b, l, -1)

@@ -1,0 +1,271 @@
+from contextlib import ExitStack
+
+import concourse.mybir as mybir
+from concourse.masks import make_identity
+
+F32 = mybir.dt.float32
+BF16 = mybir.dt.bfloat16
+U32 = mybir.dt.uint32
+U8 = mybir.dt.uint8
+FP8X4 = mybir.dt.float8_e4m3fn_x4
+ALU = mybir.AluOpType
+ACT = mybir.ActivationFunctionType
+
+P = 128
+TOKENS = 16 * 128
+E = 2048
+PACK = 4
+PASSES = E // (P * PACK)
+WORDS = P
+BANK_PLANES = 4
+HALVES = E // 2 // (WORDS * BANK_PLANES)
+SLOTS = 4
+GROUPS = TOKENS // (P * SLOTS)
+CHUNK_SLOTS = 2
+CHUNKS = SLOTS // CHUNK_SLOTS
+SAMPLE_PARTITIONS = P // SLOTS
+SAMPLE_SIZE = 128 * 128
+EPS = 1e-5
+
+FLOPS = 2 * TOKENS * E * P + 2 * TOKENS * P * P
+
+
+def tile_parallelretention_pb_kernel(tc, x, Wq, bq, kv, decay_mask, out):
+    nc = tc.nc
+    x_slots = x.flatten_outer_dims().rearrange("(g p s) k -> g p s k", p=P, s=SLOTS)
+    kv_slots = kv.flatten_outer_dims().rearrange("(g p s) k -> p g s k", p=P, s=SLOTS)
+    out_slots = out.flatten_outer_dims().rearrange("(g p s) q -> g p s q", p=P, s=SLOTS)
+
+    with ExitStack() as ctx:
+        ctx.enter_context(tc.manual_schedule())
+        const = ctx.enter_context(tc.tile_pool(name="const", bufs=1))
+        x_pool = ctx.enter_context(tc.tile_pool(name="x_pool", bufs=GROUPS * CHUNKS))
+        grouped_pool = ctx.enter_context(tc.tile_pool(name="grouped_pool", bufs=3))
+        mx_pool = ctx.enter_context(tc.tile_pool(name="mx_pool", bufs=6))
+        work = ctx.enter_context(tc.tile_pool(name="work", bufs=3))
+        small = ctx.enter_context(tc.tile_pool(name="small", bufs=3))
+        ring = ctx.enter_context(tc.psum_pool(name="ring", bufs=4))
+        q_psum = ctx.enter_context(tc.psum_pool(name="q_psum", bufs=2))
+        g_psum = ctx.enter_context(tc.psum_pool(name="g_psum", bufs=1))
+        sum_psum = ctx.enter_context(tc.psum_pool(name="sum_psum", bufs=1))
+
+        wq_rows = const.tile([P, E], BF16)
+        decay_rows = const.tile([P, P], BF16)
+        bias_rows = const.tile([P, P], BF16)
+        kv_rows = const.tile([P, GROUPS, SLOTS, P], BF16)
+        x_rows = {}
+
+        def load_chunk(g, c):
+            rows = x_pool.tile([P, CHUNK_SLOTS, E], BF16, name="x_chunk")
+            first = c * CHUNK_SLOTS
+            nc.sync.dma_start(out=rows[:], in_=x_slots[g][:, first : first + CHUNK_SLOTS, :])
+            x_rows[(g, c)] = rows
+
+        nc.vector.memset(bias_rows[:], 0.0)
+        nc.sync.dma_start(out=wq_rows[:], in_=Wq)
+        load_chunk(0, 0)
+        nc.sync.dma_start(out=decay_rows[:], in_=decay_mask.flatten_outer_dims())
+        nc.sync.dma_start(out=bias_rows[0:1, :], in_=bq.unsqueeze(0))
+        nc.sync.dma_start(out=kv_rows[:], in_=kv_slots)
+        for g in range(GROUPS):
+            for c in range(CHUNKS):
+                if (g, c) != (0, 0):
+                    load_chunk(g, c)
+
+        ident_f32 = const.tile([P, P], F32)
+        make_identity(nc, ident_f32[:])
+        ident_bf16 = const.tile([P, P], BF16)
+        make_identity(nc, ident_bf16[:])
+        ones_bf16 = const.tile([P, P], BF16)
+        nc.vector.memset(ones_bf16[:], 1.0)
+        eps_column = const.tile([P, 1], F32)
+        nc.vector.memset(eps_column[:], EPS)
+        sample_mean = const.tile([P, P], F32)
+        nc.vector.memset(sample_mean[:], 0.0)
+        for n in range(SLOTS):
+            rows = slice(n * SAMPLE_PARTITIONS, (n + 1) * SAMPLE_PARTITIONS)
+            nc.vector.memset(sample_mean[rows, rows], 1.0 / SAMPLE_SIZE)
+        table_warmer = const.tile([P, 1], F32)
+        nc.scalar.activation(out=table_warmer[:], in_=eps_column[:], func=ACT.Sqrt)
+
+        def transpose_words(words):
+            banks = []
+            for half in range(HALVES):
+                bank = ring.tile([P, BANK_PLANES, P], F32, name="word_bank", tag="ring")
+                for plane in range(BANK_PLANES):
+                    first = (half * BANK_PLANES + plane) * WORDS
+                    nc.tensor.transpose(bank[:, plane, :], words[:, first : first + WORDS], ident_f32[:])
+                banks.append(bank)
+            return banks
+
+        def regroup(banks):
+            grouped = grouped_pool.tile([P, PASSES, P, PACK], BF16, name="grouped", align_bytes=64)
+            passes_per_bank = PASSES // HALVES
+            for half in range(HALVES):
+                first = half * passes_per_bank
+                nc.scalar.copy(
+                    out=grouped[:].bitcast(F32)[:, first : first + passes_per_bank, :, :],
+                    in_=banks[half][:].rearrange("p (g u) r -> p g r u", u=PACK // 2),
+                )
+            return grouped
+
+        def quantise(grouped, codes, scales):
+            nc.vector.quantize_mx(
+                out=codes[:].bitcast(FP8X4),
+                scales=scales[:],
+                in_=grouped[:].rearrange("p g r t -> p (g r t)"),
+            )
+
+        wq_codes = const.tile([P, PASSES * P], U32, align_bytes=64)
+        wq_scales = const.tile([P, PASSES * P], U8, align_bytes=64)
+        quantise(regroup(transpose_words(wq_rows[:].bitcast(F32))), wq_codes, wq_scales)
+
+        word_banks = {}
+        x_mx = {}
+        q_bank = {}
+        g_bank = {}
+        y_tile = {}
+        row_sums = {}
+        sums_bank = {}
+        mean_column = {}
+        square_sums = {}
+        kv_t = const.tile([P, GROUPS, SLOTS, P], BF16)
+        decay_t = const.tile([P, P], BF16)
+        bias_all = const.tile([P, P], F32)
+
+        def live(g):
+            return 0 <= g < GROUPS
+
+        def prepare_kv():
+            groups_per_bank = 2
+            for first in range(0, GROUPS, groups_per_bank):
+                kv_bank = ring.tile([P, groups_per_bank, SLOTS, P], BF16, name="kv_bank", tag="ring")
+                for g in range(groups_per_bank):
+                    for s in range(SLOTS):
+                        nc.tensor.transpose(kv_bank[:, g, s, :], kv_rows[:, first + g, s, :], ident_bf16[:])
+                nc.vector.tensor_copy(out=kv_t[:, first : first + groups_per_bank, :, :], in_=kv_bank[:])
+            decay_bank = ring.tile([P, P], BF16, name="decay_bank", tag="ring")
+            nc.tensor.transpose(decay_bank[:], decay_rows[:], ident_bf16[:])
+            nc.vector.tensor_copy(out=decay_t[:], in_=decay_bank[:])
+            bias_bank = ring.tile([P, P], F32, name="bias_bank", tag="ring")
+            nc.tensor.matmul(out=bias_bank[:], lhsT=ones_bf16[:], rhs=bias_rows[:], start=True, stop=True)
+            nc.vector.tensor_copy(out=bias_all[:], in_=bias_bank[:])
+
+        def transposes(g, c):
+            if live(g):
+                for j in range(CHUNK_SLOTS):
+                    word_banks[(g, c, j)] = transpose_words(x_rows[(g, c)][:].bitcast(F32)[:, j, :])
+
+        def pack(g, c, j):
+            if live(g):
+                codes = mx_pool.tile([P, PASSES * P], U32, name="x_codes", align_bytes=64)
+                scales = mx_pool.tile([P, PASSES * P], U8, name="x_scales", align_bytes=64)
+                quantise(regroup(word_banks[(g, c, j)]), codes, scales)
+                x_mx[(g, c, j)] = (codes, scales)
+
+        def products(g, c):
+            if not live(g):
+                return
+            if c == 0:
+                q_bank[g] = q_psum.tile([P, SLOTS, P], F32, name="q_bank")
+                g_bank[g] = g_psum.tile([P, SLOTS, P], F32, name="g_bank")
+            for j in range(CHUNK_SLOTS):
+                codes, scales = x_mx[(g, c, j)]
+                for k_pass in range(PASSES):
+                    cols = slice(k_pass * P, (k_pass + 1) * P)
+                    nc.tensor.matmul_mx(
+                        out=q_bank[g][:, c * CHUNK_SLOTS + j, :],
+                        lhsT=codes[:, cols].bitcast(FP8X4),
+                        lhsT_scale=scales[:, cols],
+                        rhs=wq_codes[:, cols].bitcast(FP8X4),
+                        rhs_scale=wq_scales[:, cols],
+                        start=(k_pass == 0),
+                        stop=(k_pass == PASSES - 1),
+                    )
+            for j in range(CHUNK_SLOTS):
+                s = c * CHUNK_SLOTS + j
+                nc.tensor.matmul(out=g_bank[g][:, s, :], lhsT=kv_t[:, g, s, :], rhs=decay_t[:], start=True, stop=True)
+
+        def weigh(g, c):
+            if not live(g):
+                return
+            if c == 0:
+                y_tile[g] = work.tile([P, SLOTS, P], F32, name="y_tile")
+                row_sums[g] = small.tile([P, CHUNKS], F32, name="row_sums")
+            slots = slice(c * CHUNK_SLOTS, (c + 1) * CHUNK_SLOTS)
+            biased = work.tile([P, CHUNK_SLOTS, P], F32, name="biased")
+            nc.vector.tensor_tensor(
+                out=biased[:],
+                in0=q_bank[g][:, slots, :],
+                in1=bias_all[:].unsqueeze(1).to_broadcast([P, CHUNK_SLOTS, P]),
+                op=ALU.add,
+            )
+            nc.vector.scalar_tensor_tensor(
+                out=y_tile[g][:, slots, :].rearrange("p s q -> p (s q)"),
+                in0=biased[:].rearrange("p s q -> p (s q)"),
+                scalar=1.0,
+                in1=g_bank[g][:, slots, :].rearrange("p s q -> p (s q)"),
+                op0=ALU.mult,
+                op1=ALU.mult,
+                accum_out=row_sums[g][:, c : c + 1],
+            )
+
+        def mean_of(g):
+            if not live(g):
+                return
+            sums_bank[g] = sum_psum.tile([P, CHUNKS + 1], F32, name="sums_bank")
+            nc.tensor.matmul(out=sums_bank[g][:, 0:CHUNKS], lhsT=sample_mean[:], rhs=row_sums[g][:], start=True, stop=True)
+            mean_column[g] = small.tile([P, 1], F32, name="mean_column")
+            nc.vector.tensor_reduce(out=mean_column[g][:], in_=sums_bank[g][:, 0:CHUNKS], axis=mybir.AxisListType.X, op=ALU.add)
+
+        def squares(g):
+            if not live(g):
+                return
+            squared = work.tile([P, SLOTS * P], F32, name="squared")
+            square_sums[g] = small.tile([P, 1], F32, name="square_sums")
+            nc.scalar.activation(
+                out=squared[:],
+                in_=y_tile[g][:].rearrange("p s q -> p (s q)"),
+                func=ACT.Square,
+                bias=mean_column[g][:],
+                scale=-1.0,
+                accum_out=square_sums[g][:],
+            )
+
+        def variance_of(g):
+            if live(g):
+                nc.tensor.matmul(
+                    out=sums_bank[g][:, CHUNKS : CHUNKS + 1], lhsT=sample_mean[:], rhs=square_sums[g][:], start=True, stop=True
+                )
+
+        def finish(g):
+            if not live(g):
+                return
+            std = small.tile([P, 1], F32, name="std")
+            nc.scalar.activation(out=std[:], in_=sums_bank[g][:, CHUNKS : CHUNKS + 1], func=ACT.Sqrt, bias=eps_column[:])
+            rstd = small.tile([P, 1], F32, name="rstd")
+            nc.vector.reciprocal(out=rstd[:], in_=std[:])
+            res = work.tile([P, SLOTS, P], F32, name="res")
+            nc.vector.tensor_scalar(
+                out=res[:], in0=y_tile[g][:], scalar1=mean_column[g][:], scalar2=rstd[:], op0=ALU.subtract, op1=ALU.mult
+            )
+            nc.sync.dma_start(out=out_slots[g], in_=res[:])
+
+        for i in range(GROUPS + 2):
+            transposes(i, 0)
+            variance_of(i - 2)
+            products(i - 1, 1)
+            pack(i, 0, 0)
+            weigh(i - 1, 1)
+            pack(i, 0, 1)
+            finish(i - 2)
+            if i == 0:
+                prepare_kv()
+
+            transposes(i, 1)
+            mean_of(i - 1)
+            products(i, 0)
+            pack(i, 1, 0)
+            squares(i - 1)
+            weigh(i, 0)
+            pack(i, 1, 1)

@@ -37,7 +37,6 @@ def tile_parallelretention_pb_kernel(tc, x, Wq, bq, kv, decay_mask, out):
     out_slots = out.flatten_outer_dims().rearrange("(g p s) q -> g p s q", p=P, s=SLOTS)
 
     with ExitStack() as ctx:
-        ctx.enter_context(tc.manual_schedule())
         const = ctx.enter_context(tc.tile_pool(name="const", bufs=1))
         x_pool = ctx.enter_context(tc.tile_pool(name="x_pool", bufs=GROUPS * CHUNKS))
         grouped_pool = ctx.enter_context(tc.tile_pool(name="grouped_pool", bufs=3))

@@ -26,6 +26,7 @@ CHUNKS = SLOTS // CHUNK_SLOTS
 SAMPLE_PARTITIONS = P // SLOTS
 SAMPLE_SIZE = 128 * 128
 EPS = 1e-5
+VECTOR_SHARE = 8
 
 FLOPS = 2 * TOKENS * E * P + 2 * TOKENS * P * P
 
@@ -38,14 +39,13 @@ def tile_parallelretention_pb_kernel(tc, x, Wq, bq, kv, decay_mask, out):
 
     with ExitStack() as ctx:
         const = ctx.enter_context(tc.tile_pool(name="const", bufs=1))
-        x_pool = ctx.enter_context(tc.tile_pool(name="x_pool", bufs=GROUPS * CHUNKS))
+        x_pool = ctx.enter_context(tc.tile_pool(name="x_pool", bufs=GROUPS * SLOTS))
         grouped_pool = ctx.enter_context(tc.tile_pool(name="grouped_pool", bufs=3))
         mx_pool = ctx.enter_context(tc.tile_pool(name="mx_pool", bufs=6))
         work = ctx.enter_context(tc.tile_pool(name="work", bufs=3))
         small = ctx.enter_context(tc.tile_pool(name="small", bufs=3))
-        ring = ctx.enter_context(tc.psum_pool(name="ring", bufs=4))
-        q_psum = ctx.enter_context(tc.psum_pool(name="q_psum", bufs=2))
-        g_psum = ctx.enter_context(tc.psum_pool(name="g_psum", bufs=1))
+        ring = ctx.enter_context(tc.psum_pool(name="ring", bufs=5))
+        qg_psum = ctx.enter_context(tc.psum_pool(name="qg_psum", bufs=2))
         sum_psum = ctx.enter_context(tc.psum_pool(name="sum_psum", bufs=1))
 
         wq_rows = const.tile([P, E], BF16)
@@ -54,22 +54,22 @@ def tile_parallelretention_pb_kernel(tc, x, Wq, bq, kv, decay_mask, out):
         kv_rows = const.tile([P, GROUPS, SLOTS, P], BF16)
         x_rows = {}
 
-        def load_chunk(g, c):
-            rows = x_pool.tile([P, CHUNK_SLOTS, E], BF16, name="x_chunk")
-            first = c * CHUNK_SLOTS
-            nc.sync.dma_start(out=rows[:], in_=x_slots[g][:, first : first + CHUNK_SLOTS, :])
-            x_rows[(g, c)] = rows
+        def load_token_tile(g, s):
+            rows = x_pool.tile([P, E], BF16, name="x_tile")
+            nc.sync.dma_start(out=rows[:], in_=x_slots[g][:, s, :])
+            x_rows[(g, s)] = rows
 
         nc.vector.memset(bias_rows[:], 0.0)
         nc.sync.dma_start(out=wq_rows[:], in_=Wq)
-        load_chunk(0, 0)
+        load_token_tile(0, 0)
+        load_token_tile(0, 1)
         nc.sync.dma_start(out=decay_rows[:], in_=decay_mask.flatten_outer_dims())
         nc.sync.dma_start(out=bias_rows[0:1, :], in_=bq.unsqueeze(0))
         nc.sync.dma_start(out=kv_rows[:], in_=kv_slots)
         for g in range(GROUPS):
-            for c in range(CHUNKS):
-                if (g, c) != (0, 0):
-                    load_chunk(g, c)
+            for s in range(SLOTS):
+                if (g, s) not in x_rows:
+                    load_token_tile(g, s)
 
         ident_f32 = const.tile([P, P], F32)
         make_identity(nc, ident_f32[:])
@@ -85,7 +85,9 @@ def tile_parallelretention_pb_kernel(tc, x, Wq, bq, kv, decay_mask, out):
             rows = slice(n * SAMPLE_PARTITIONS, (n + 1) * SAMPLE_PARTITIONS)
             nc.vector.memset(sample_mean[rows, rows], 1.0 / SAMPLE_SIZE)
         table_warmer = const.tile([P, 1], F32)
-        nc.scalar.activation(out=table_warmer[:], in_=eps_column[:], func=ACT.Sqrt)
+        nc.scalar.activation(out=table_warmer[:], in_=eps_column[:], func=ACT.Abs_reciprocal_sqrt)
+
+        banks_emptied = []
 
         def transpose_words(words):
             banks = []
@@ -102,10 +104,13 @@ def tile_parallelretention_pb_kernel(tc, x, Wq, bq, kv, decay_mask, out):
             passes_per_bank = PASSES // HALVES
             for half in range(HALVES):
                 first = half * passes_per_bank
-                nc.scalar.copy(
-                    out=grouped[:].bitcast(F32)[:, first : first + passes_per_bank, :, :],
-                    in_=banks[half][:].rearrange("p (g u) r -> p g r u", u=PACK // 2),
-                )
+                side_by_side = grouped[:].bitcast(F32)[:, first : first + passes_per_bank, :, :]
+                planes = banks[half][:].rearrange("p (g u) r -> p g r u", u=PACK // 2)
+                banks_emptied.append(half)
+                if len(banks_emptied) % VECTOR_SHARE == 0:
+                    nc.vector.tensor_copy(out=side_by_side, in_=planes)
+                else:
+                    nc.scalar.copy(out=side_by_side, in_=planes)
             return grouped
 
         def quantise(grouped, codes, scales):
@@ -153,7 +158,7 @@ def tile_parallelretention_pb_kernel(tc, x, Wq, bq, kv, decay_mask, out):
         def transposes(g, c):
             if live(g):
                 for j in range(CHUNK_SLOTS):
-                    word_banks[(g, c, j)] = transpose_words(x_rows[(g, c)][:].bitcast(F32)[:, j, :])
+                    word_banks[(g, c, j)] = transpose_words(x_rows[(g, c * CHUNK_SLOTS + j)][:].bitcast(F32))
 
         def pack(g, c, j):
             if live(g):
@@ -165,15 +170,15 @@ def tile_parallelretention_pb_kernel(tc, x, Wq, bq, kv, decay_mask, out):
         def products(g, c):
             if not live(g):
                 return
-            if c == 0:
-                q_bank[g] = q_psum.tile([P, SLOTS, P], F32, name="q_bank")
-                g_bank[g] = g_psum.tile([P, SLOTS, P], F32, name="g_bank")
+            qg_bank = qg_psum.tile([P, 2, CHUNK_SLOTS, P], F32, name="qg_bank")
+            q_bank[(g, c)] = qg_bank[:, 0, :, :]
+            g_bank[(g, c)] = qg_bank[:, 1, :, :]
             for j in range(CHUNK_SLOTS):
                 codes, scales = x_mx[(g, c, j)]
                 for k_pass in range(PASSES):
                     cols = slice(k_pass * P, (k_pass + 1) * P)
                     nc.tensor.matmul_mx(
-                        out=q_bank[g][:, c * CHUNK_SLOTS + j, :],
+                        out=q_bank[(g, c)][:, j, :],
                         lhsT=codes[:, cols].bitcast(FP8X4),
                         lhsT_scale=scales[:, cols],
                         rhs=wq_codes[:, cols].bitcast(FP8X4),
@@ -182,8 +187,9 @@ def tile_parallelretention_pb_kernel(tc, x, Wq, bq, kv, decay_mask, out):
                         stop=(k_pass == PASSES - 1),
                     )
             for j in range(CHUNK_SLOTS):
-                s = c * CHUNK_SLOTS + j
-                nc.tensor.matmul(out=g_bank[g][:, s, :], lhsT=kv_t[:, g, s, :], rhs=decay_t[:], start=True, stop=True)
+                nc.tensor.matmul(
+                    out=g_bank[(g, c)][:, j, :], lhsT=kv_t[:, g, c * CHUNK_SLOTS + j, :], rhs=decay_t[:], start=True, stop=True
+                )
 
         def weigh(g, c):
             if not live(g):
@@ -195,7 +201,7 @@ def tile_parallelretention_pb_kernel(tc, x, Wq, bq, kv, decay_mask, out):
             biased = work.tile([P, CHUNK_SLOTS, P], F32, name="biased")
             nc.vector.tensor_tensor(
                 out=biased[:],
-                in0=q_bank[g][:, slots, :],
+                in0=q_bank[(g, c)],
                 in1=bias_all[:].unsqueeze(1).to_broadcast([P, CHUNK_SLOTS, P]),
                 op=ALU.add,
             )
@@ -203,7 +209,7 @@ def tile_parallelretention_pb_kernel(tc, x, Wq, bq, kv, decay_mask, out):
                 out=y_tile[g][:, slots, :].rearrange("p s q -> p (s q)"),
                 in0=biased[:].rearrange("p s q -> p (s q)"),
                 scalar=1.0,
-                in1=g_bank[g][:, slots, :].rearrange("p s q -> p (s q)"),
+                in1=g_bank[(g, c)].rearrange("p s q -> p (s q)"),
                 op0=ALU.mult,
                 op1=ALU.mult,
                 accum_out=row_sums[g][:, c : c + 1],
@@ -240,10 +246,10 @@ def tile_parallelretention_pb_kernel(tc, x, Wq, bq, kv, decay_mask, out):
         def finish(g):
             if not live(g):
                 return
-            std = small.tile([P, 1], F32, name="std")
-            nc.scalar.activation(out=std[:], in_=sums_bank[g][:, CHUNKS : CHUNKS + 1], func=ACT.Sqrt, bias=eps_column[:])
             rstd = small.tile([P, 1], F32, name="rstd")
-            nc.vector.reciprocal(out=rstd[:], in_=std[:])
+            nc.scalar.activation(
+                out=rstd[:], in_=sums_bank[g][:, CHUNKS : CHUNKS + 1], func=ACT.Abs_reciprocal_sqrt, bias=eps_column[:]
+            )
             res = work.tile([P, SLOTS, P], F32, name="res")
             nc.vector.tensor_scalar(
                 out=res[:], in0=y_tile[g][:], scalar1=mean_column[g][:], scalar2=rstd[:], op0=ALU.subtract, op1=ALU.mult

@@ -26,6 +26,7 @@ CHUNKS = SLOTS // CHUNK_SLOTS
 SAMPLE_PARTITIONS = P // SLOTS
 SAMPLE_SIZE = 128 * 128
 EPS = 1e-5
+CLOCK_PASSES = 2
 VECTOR_SHARE = 8
 
 FLOPS = 2 * TOKENS * E * P + 2 * TOKENS * P * P
@@ -38,13 +39,15 @@ def tile_parallelretention_pb_kernel(tc, x, Wq, bq, kv, decay_mask, out):
     out_slots = out.flatten_outer_dims().rearrange("(g p s) q -> g p s q", p=P, s=SLOTS)
 
     with ExitStack() as ctx:
+        ctx.enter_context(tc.manual_schedule())
         const = ctx.enter_context(tc.tile_pool(name="const", bufs=1))
         x_pool = ctx.enter_context(tc.tile_pool(name="x_pool", bufs=GROUPS * SLOTS))
         grouped_pool = ctx.enter_context(tc.tile_pool(name="grouped_pool", bufs=3))
         mx_pool = ctx.enter_context(tc.tile_pool(name="mx_pool", bufs=6))
         work = ctx.enter_context(tc.tile_pool(name="work", bufs=3))
         small = ctx.enter_context(tc.tile_pool(name="small", bufs=3))
-        ring = ctx.enter_context(tc.psum_pool(name="ring", bufs=5))
+        ring = ctx.enter_context(tc.psum_pool(name="ring", bufs=4))
+        unread_psum = ctx.enter_context(tc.psum_pool(name="unread_psum", bufs=1))
         qg_psum = ctx.enter_context(tc.psum_pool(name="qg_psum", bufs=2))
         sum_psum = ctx.enter_context(tc.psum_pool(name="sum_psum", bufs=1))
 
@@ -186,6 +189,17 @@ def tile_parallelretention_pb_kernel(tc, x, Wq, bq, kv, decay_mask, out):
                         start=(k_pass == 0),
                         stop=(k_pass == PASSES - 1),
                     )
+            for clock_pass in range(CLOCK_PASSES):
+                unread = unread_psum.tile([P, PASSES * P], F32, name="unread")
+                nc.tensor.matmul_mx(
+                    out=unread[:],
+                    lhsT=wq_codes[:, 0:P].bitcast(FP8X4),
+                    lhsT_scale=wq_scales[:, 0:P],
+                    rhs=wq_codes[:].bitcast(FP8X4),
+                    rhs_scale=wq_scales[:],
+                    start=True,
+                    stop=True,
+                )
             for j in range(CHUNK_SLOTS):
                 nc.tensor.matmul(
                     out=g_bank[(g, c)][:, j, :], lhsT=kv_t[:, g, c * CHUNK_SLOTS + j, :], rhs=decay_t[:], start=True, stop=True
@@ -271,6 +285,6 @@ def tile_parallelretention_pb_kernel(tc, x, Wq, bq, kv, decay_mask, out):
             mean_of(i - 1)
             products(i, 0)
             pack(i, 1, 0)
-            squares(i - 1)
             weigh(i, 0)
             pack(i, 1, 1)
+            squares(i - 1)

from contextlib import ExitStack

import concourse.mybir as mybir
from concourse.masks import make_identity

F32 = mybir.dt.float32
BF16 = mybir.dt.bfloat16
U32 = mybir.dt.uint32
U8 = mybir.dt.uint8
FP8X4 = mybir.dt.float8_e4m3fn_x4
ALU = mybir.AluOpType
ACT = mybir.ActivationFunctionType

P = 128
TOKENS = 16 * 128
E = 2048
PACK = 4
PASSES = E // (P * PACK)
WORDS = P
BANK_PLANES = 4
HALVES = E // 2 // (WORDS * BANK_PLANES)
SLOTS = 4
GROUPS = TOKENS // (P * SLOTS)
CHUNK_SLOTS = 2
CHUNKS = SLOTS // CHUNK_SLOTS
SAMPLE_PARTITIONS = P // SLOTS
SAMPLE_SIZE = 128 * 128
EPS = 1e-5
CLOCK_PASSES = 2
VECTOR_SHARE = 8

FLOPS = 2 * TOKENS * E * P + 2 * TOKENS * P * P


def tile_parallelretention_pb_kernel(tc, x, Wq, bq, kv, decay_mask, out):
    nc = tc.nc
    x_slots = x.flatten_outer_dims().rearrange("(g p s) k -> g p s k", p=P, s=SLOTS)
    kv_slots = kv.flatten_outer_dims().rearrange("(g p s) k -> p g s k", p=P, s=SLOTS)
    out_slots = out.flatten_outer_dims().rearrange("(g p s) q -> g p s q", p=P, s=SLOTS)

    with ExitStack() as ctx:
        ctx.enter_context(tc.manual_schedule())
        const = ctx.enter_context(tc.tile_pool(name="const", bufs=1))
        x_pool = ctx.enter_context(tc.tile_pool(name="x_pool", bufs=GROUPS * SLOTS))
        grouped_pool = ctx.enter_context(tc.tile_pool(name="grouped_pool", bufs=3))
        mx_pool = ctx.enter_context(tc.tile_pool(name="mx_pool", bufs=6))
        work = ctx.enter_context(tc.tile_pool(name="work", bufs=3))
        small = ctx.enter_context(tc.tile_pool(name="small", bufs=3))
        ring = ctx.enter_context(tc.psum_pool(name="ring", bufs=4))
        unread_psum = ctx.enter_context(tc.psum_pool(name="unread_psum", bufs=1))
        qg_psum = ctx.enter_context(tc.psum_pool(name="qg_psum", bufs=2))
        sum_psum = ctx.enter_context(tc.psum_pool(name="sum_psum", bufs=1))

        wq_rows = const.tile([P, E], BF16)
        decay_rows = const.tile([P, P], BF16)
        bias_rows = const.tile([P, P], BF16)
        kv_rows = const.tile([P, GROUPS, SLOTS, P], BF16)
        x_rows = {}

        def load_token_tile(g, s):
            rows = x_pool.tile([P, E], BF16, name="x_tile")
            nc.sync.dma_start(out=rows[:], in_=x_slots[g][:, s, :])
            x_rows[(g, s)] = rows

        nc.vector.memset(bias_rows[:], 0.0)
        nc.sync.dma_start(out=wq_rows[:], in_=Wq)
        load_token_tile(0, 0)
        load_token_tile(0, 1)
        nc.sync.dma_start(out=decay_rows[:], in_=decay_mask.flatten_outer_dims())
        nc.sync.dma_start(out=bias_rows[0:1, :], in_=bq.unsqueeze(0))
        nc.sync.dma_start(out=kv_rows[:], in_=kv_slots)
        for g in range(GROUPS):
            for s in range(SLOTS):
                if (g, s) not in x_rows:
                    load_token_tile(g, s)

        ident_f32 = const.tile([P, P], F32)
        make_identity(nc, ident_f32[:])
        ident_bf16 = const.tile([P, P], BF16)
        make_identity(nc, ident_bf16[:])
        ones_bf16 = const.tile([P, P], BF16)
        nc.vector.memset(ones_bf16[:], 1.0)
        eps_column = const.tile([P, 1], F32)
        nc.vector.memset(eps_column[:], EPS)
        sample_mean = const.tile([P, P], F32)
        nc.vector.memset(sample_mean[:], 0.0)
        for n in range(SLOTS):
            rows = slice(n * SAMPLE_PARTITIONS, (n + 1) * SAMPLE_PARTITIONS)
            nc.vector.memset(sample_mean[rows, rows], 1.0 / SAMPLE_SIZE)
        table_warmer = const.tile([P, 1], F32)
        nc.scalar.activation(out=table_warmer[:], in_=eps_column[:], func=ACT.Abs_reciprocal_sqrt)

        banks_emptied = []

        def transpose_words(words):
            banks = []
            for half in range(HALVES):
                bank = ring.tile([P, BANK_PLANES, P], F32, name="word_bank", tag="ring")
                for plane in range(BANK_PLANES):
                    first = (half * BANK_PLANES + plane) * WORDS
                    nc.tensor.transpose(bank[:, plane, :], words[:, first : first + WORDS], ident_f32[:])
                banks.append(bank)
            return banks

        def regroup(banks):
            grouped = grouped_pool.tile([P, PASSES, P, PACK], BF16, name="grouped", align_bytes=64)
            passes_per_bank = PASSES // HALVES
            for half in range(HALVES):
                first = half * passes_per_bank
                side_by_side = grouped[:].bitcast(F32)[:, first : first + passes_per_bank, :, :]
                planes = banks[half][:].rearrange("p (g u) r -> p g r u", u=PACK // 2)
                banks_emptied.append(half)
                if len(banks_emptied) % VECTOR_SHARE == 0:
                    nc.vector.tensor_copy(out=side_by_side, in_=planes)
                else:
                    nc.scalar.copy(out=side_by_side, in_=planes)
            return grouped

        def quantise(grouped, codes, scales):
            nc.vector.quantize_mx(
                out=codes[:].bitcast(FP8X4),
                scales=scales[:],
                in_=grouped[:].rearrange("p g r t -> p (g r t)"),
            )

        wq_codes = const.tile([P, PASSES * P], U32, align_bytes=64)
        wq_scales = const.tile([P, PASSES * P], U8, align_bytes=64)
        quantise(regroup(transpose_words(wq_rows[:].bitcast(F32))), wq_codes, wq_scales)

        word_banks = {}
        x_mx = {}
        q_bank = {}
        g_bank = {}
        y_tile = {}
        row_sums = {}
        sums_bank = {}
        mean_column = {}
        square_sums = {}
        kv_t = const.tile([P, GROUPS, SLOTS, P], BF16)
        decay_t = const.tile([P, P], BF16)
        bias_all = const.tile([P, P], F32)

        def live(g):
            return 0 <= g < GROUPS

        def prepare_kv():
            groups_per_bank = 2
            for first in range(0, GROUPS, groups_per_bank):
                kv_bank = ring.tile([P, groups_per_bank, SLOTS, P], BF16, name="kv_bank", tag="ring")
                for g in range(groups_per_bank):
                    for s in range(SLOTS):
                        nc.tensor.transpose(kv_bank[:, g, s, :], kv_rows[:, first + g, s, :], ident_bf16[:])
                nc.vector.tensor_copy(out=kv_t[:, first : first + groups_per_bank, :, :], in_=kv_bank[:])
            decay_bank = ring.tile([P, P], BF16, name="decay_bank", tag="ring")
            nc.tensor.transpose(decay_bank[:], decay_rows[:], ident_bf16[:])
            nc.vector.tensor_copy(out=decay_t[:], in_=decay_bank[:])
            bias_bank = ring.tile([P, P], F32, name="bias_bank", tag="ring")
            nc.tensor.matmul(out=bias_bank[:], lhsT=ones_bf16[:], rhs=bias_rows[:], start=True, stop=True)
            nc.vector.tensor_copy(out=bias_all[:], in_=bias_bank[:])

        def transposes(g, c):
            if live(g):
                for j in range(CHUNK_SLOTS):
                    word_banks[(g, c, j)] = transpose_words(x_rows[(g, c * CHUNK_SLOTS + j)][:].bitcast(F32))

        def pack(g, c, j):
            if live(g):
                codes = mx_pool.tile([P, PASSES * P], U32, name="x_codes", align_bytes=64)
                scales = mx_pool.tile([P, PASSES * P], U8, name="x_scales", align_bytes=64)
                quantise(regroup(word_banks[(g, c, j)]), codes, scales)
                x_mx[(g, c, j)] = (codes, scales)

        def products(g, c):
            if not live(g):
                return
            qg_bank = qg_psum.tile([P, 2, CHUNK_SLOTS, P], F32, name="qg_bank")
            q_bank[(g, c)] = qg_bank[:, 0, :, :]
            g_bank[(g, c)] = qg_bank[:, 1, :, :]
            for j in range(CHUNK_SLOTS):
                codes, scales = x_mx[(g, c, j)]
                for k_pass in range(PASSES):
                    cols = slice(k_pass * P, (k_pass + 1) * P)
                    nc.tensor.matmul_mx(
                        out=q_bank[(g, c)][:, j, :],
                        lhsT=codes[:, cols].bitcast(FP8X4),
                        lhsT_scale=scales[:, cols],
                        rhs=wq_codes[:, cols].bitcast(FP8X4),
                        rhs_scale=wq_scales[:, cols],
                        start=(k_pass == 0),
                        stop=(k_pass == PASSES - 1),
                    )
            for clock_pass in range(CLOCK_PASSES):
                unread = unread_psum.tile([P, PASSES * P], F32, name="unread")
                nc.tensor.matmul_mx(
                    out=unread[:],
                    lhsT=wq_codes[:, 0:P].bitcast(FP8X4),
                    lhsT_scale=wq_scales[:, 0:P],
                    rhs=wq_codes[:].bitcast(FP8X4),
                    rhs_scale=wq_scales[:],
                    start=True,
                    stop=True,
                )
            for j in range(CHUNK_SLOTS):
                nc.tensor.matmul(
                    out=g_bank[(g, c)][:, j, :], lhsT=kv_t[:, g, c * CHUNK_SLOTS + j, :], rhs=decay_t[:], start=True, stop=True
                )

        def weigh(g, c):
            if not live(g):
                return
            if c == 0:
                y_tile[g] = work.tile([P, SLOTS, P], F32, name="y_tile")
                row_sums[g] = small.tile([P, CHUNKS], F32, name="row_sums")
            slots = slice(c * CHUNK_SLOTS, (c + 1) * CHUNK_SLOTS)
            biased = work.tile([P, CHUNK_SLOTS, P], F32, name="biased")
            nc.vector.tensor_tensor(
                out=biased[:],
                in0=q_bank[(g, c)],
                in1=bias_all[:].unsqueeze(1).to_broadcast([P, CHUNK_SLOTS, P]),
                op=ALU.add,
            )
            nc.vector.scalar_tensor_tensor(
                out=y_tile[g][:, slots, :].rearrange("p s q -> p (s q)"),
                in0=biased[:].rearrange("p s q -> p (s q)"),
                scalar=1.0,
                in1=g_bank[(g, c)].rearrange("p s q -> p (s q)"),
                op0=ALU.mult,
                op1=ALU.mult,
                accum_out=row_sums[g][:, c : c + 1],
            )

        def mean_of(g):
            if not live(g):
                return
            sums_bank[g] = sum_psum.tile([P, CHUNKS + 1], F32, name="sums_bank")
            nc.tensor.matmul(out=sums_bank[g][:, 0:CHUNKS], lhsT=sample_mean[:], rhs=row_sums[g][:], start=True, stop=True)
            mean_column[g] = small.tile([P, 1], F32, name="mean_column")
            nc.vector.tensor_reduce(out=mean_column[g][:], in_=sums_bank[g][:, 0:CHUNKS], axis=mybir.AxisListType.X, op=ALU.add)

        def squares(g):
            if not live(g):
                return
            squared = work.tile([P, SLOTS * P], F32, name="squared")
            square_sums[g] = small.tile([P, 1], F32, name="square_sums")
            nc.scalar.activation(
                out=squared[:],
                in_=y_tile[g][:].rearrange("p s q -> p (s q)"),
                func=ACT.Square,
                bias=mean_column[g][:],
                scale=-1.0,
                accum_out=square_sums[g][:],
            )

        def variance_of(g):
            if live(g):
                nc.tensor.matmul(
                    out=sums_bank[g][:, CHUNKS : CHUNKS + 1], lhsT=sample_mean[:], rhs=square_sums[g][:], start=True, stop=True
                )

        def finish(g):
            if not live(g):
                return
            rstd = small.tile([P, 1], F32, name="rstd")
            nc.scalar.activation(
                out=rstd[:], in_=sums_bank[g][:, CHUNKS : CHUNKS + 1], func=ACT.Abs_reciprocal_sqrt, bias=eps_column[:]
            )
            res = work.tile([P, SLOTS, P], F32, name="res")
            nc.vector.tensor_scalar(
                out=res[:], in0=y_tile[g][:], scalar1=mean_column[g][:], scalar2=rstd[:], op0=ALU.subtract, op1=ALU.mult
            )
            nc.sync.dma_start(out=out_slots[g], in_=res[:])

        for i in range(GROUPS + 2):
            transposes(i, 0)
            variance_of(i - 2)
            products(i - 1, 1)
            pack(i, 0, 0)
            weigh(i - 1, 1)
            pack(i, 0, 1)
            finish(i - 2)
            if i == 0:
                prepare_kv()

            transposes(i, 1)
            mean_of(i - 1)
            products(i, 0)
            pack(i, 1, 0)
            weigh(i, 0)
            pack(i, 1, 1)
            squares(i - 1)
